import numpy as np
import ml_dtypes


def mxq(x, axis, fmt="e4m3"):
    dtype, down = {"e4m3": (ml_dtypes.float8_e4m3fn, 7), "e5m2": (ml_dtypes.float8_e5m2, 14)}[fmt]
    v = np.moveaxis(np.asarray(x, np.float32).astype(ml_dtypes.bfloat16).astype(np.float64), axis, -1)
    blocks = v.reshape(v.shape[:-1] + (-1, 32))
    amax = np.abs(blocks).max(-1, keepdims=True)
    byte = np.maximum(np.where(amax > 0, np.frexp(amax)[1] - 1 + 127, 0) - down, 1)
    scale = np.exp2(byte - 127.0)
    codes = (blocks / scale).astype(np.float32).astype(dtype).astype(np.float64)
    return np.moveaxis((codes * scale).reshape(v.shape), -1, axis)


WIDE = False


def mx_kscale(k):
    if not WIDE:
        return np.ones(k)
    levels = np.array([10, -10, 5, -5, 0])
    if k % 512:
        return np.exp2(np.random.permutation(np.resize(levels, k // 32))).repeat(32)
    a = np.empty((k // 512, 16))
    for p in range(k // 512):
        a[p, :8] = np.random.permutation(np.resize(levels, 8))
        for g in range(8):
            far = levels[np.abs(levels - a[p, g]) >= 10]
            a[p, g + 8] = far[np.random.randint(len(far))]
    return np.exp2(a.ravel()).repeat(32)


BF16 = ml_dtypes.bfloat16


def bf(x):
    return np.asarray(x, np.float32).astype(BF16)


def f64(x):
    return np.asarray(x).astype(np.float64)


B, S, D, H, DH = 2, 4096, 512, 2, 64
E = H * DH
EPS = 1e-12


def rotate_half(t):
    t1, t2 = np.split(t, 2, axis=-1)
    return np.concatenate((-t2, t1), axis=-1)


def apply_rotary(pos, t):
    return t * np.cos(pos) + rotate_half(t) * np.sin(pos)


def setup_inputs():
    s = mx_kscale(D)
    ang = np.random.uniform(-np.pi, np.pi, (S, DH // 2))
    col = np.concatenate((np.full(E, np.sqrt(3.0 / DH)), np.full(E, np.sqrt(3.0 / DH)), np.ones(E)))
    return {"x": bf(np.random.standard_normal((B, S, D))),
            "rotary_emb": bf(np.concatenate((ang, ang), axis=-1)),
            "gamma": bf((1.0 + 0.1 * np.random.standard_normal(D)) * s),
            "w_qkv": bf(np.random.standard_normal((D, 3 * E)) * col / np.sqrt(D) / s[:, None])}


def reference(x, rotary_emb, gamma, w_qkv):
    x, pos = f64(x), f64(rotary_emb)
    l2 = np.sqrt((x * x).sum(-1, keepdims=True))
    xn = x / np.maximum(l2, EPS) * np.sqrt(D) * f64(gamma)
    qkv = mxq(xn, 2, "e4m3") @ mxq(f64(w_qkv), 0, "e4m3")
    qkv = qkv.reshape(B, S, 3, H, DH).transpose(2, 0, 3, 1, 4)
    q, k, v = qkv[0], qkv[1], qkv[2]
    q = apply_rotary(pos, q)
    k = apply_rotary(pos, k)
    q = q * np.sqrt(DH)
    return q, k, v

@@ -1,0 +1,287 @@
+import math
+from contextlib import ExitStack
+
+import concourse.mybir as mybir
+from concourse.masks import make_identity
+
+F32 = mybir.dt.float32
+BF16 = mybir.dt.bfloat16
+U32 = mybir.dt.uint32
+U8 = mybir.dt.uint8
+FP8X4 = mybir.dt.float8_e4m3fn_x4
+ALU = mybir.AluOpType
+ACT = mybir.ActivationFunctionType
+
+P = 128
+BATCH, SEQ, DIM = 2, 4096, 512
+HEADS, HEAD_DIM = 2, 64
+HALF = HEAD_DIM // 2
+INNER = HEADS * HEAD_DIM
+PACK = 4
+POS_PER_PART = SEQ // P
+GROUP = 4
+GROUPS_PER_BATCH = POS_PER_PART // GROUP
+N_GROUPS = BATCH * GROUPS_PER_BATCH
+ROT_COLS = 4 * INNER
+EPS = 1e-12
+
+FLOPS = 2 * BATCH * SEQ * DIM * 3 * INNER
+
+
+def tile_ringattention_pa_t_kernel(tc, x, rotary_emb, gamma, w_qkv, out_0, out_1, out_2):
+    nc = tc.nc
+    x_rows = x.rearrange("b (p t) k -> b p t k", t=POS_PER_PART)
+    angle_rows = rotary_emb.rearrange("(p t) d -> p t d", t=POS_PER_PART)
+    q_rows = out_0.rearrange("b h (p t) d -> b p h t d", t=POS_PER_PART)
+    k_rows = out_1.rearrange("b h (p t) d -> b p h t d", t=POS_PER_PART)
+    v_rows = out_2.rearrange("b h (p t) d -> b p h t d", t=POS_PER_PART)
+
+    with ExitStack() as stack:
+        keep = stack.enter_context(tc.tile_pool(name="keep", bufs=1))
+        small = stack.enter_context(tc.tile_pool(name="small", bufs=6))
+        work = stack.enter_context(tc.tile_pool(name="work", bufs=2))
+        results = stack.enter_context(tc.tile_pool(name="results", bufs=3))
+        psum_keep = stack.enter_context(tc.psum_pool(name="psum_keep", bufs=1))
+        psum_t = stack.enter_context(tc.psum_pool(name="psum_t", bufs=2))
+        psum_rot = stack.enter_context(tc.psum_pool(name="psum_rot", bufs=4))
+        psum_v = stack.enter_context(tc.psum_pool(name="psum_v", bufs=1))
+        stack.enter_context(tc.manual_schedule())
+
+        def where(g):
+            c, b = divmod(g, BATCH)
+            return b, c * GROUP
+
+        x_all = keep.tile([P, BATCH, POS_PER_PART, DIM], BF16)
+
+        def load_x(g):
+            b, t0 = where(g)
+            for t in range(t0, t0 + GROUP, 2):
+                nc.sync.dma_start(out=x_all[:, b, t : t + 2, :], in_=x_rows[b, :, t : t + 2, :])
+
+        load_x(0)
+        gamma_row = keep.tile([P, DIM], BF16)
+        nc.vector.memset(gamma_row[:], 0.0)
+        nc.sync.dma_start(out=gamma_row[0:1, :], in_=gamma.rearrange("(o k) -> o k", o=1))
+        w_raw = keep.tile([P, PACK, 3 * INNER], BF16)
+        nc.sync.dma_start(
+            out=w_raw[:],
+            in_=w_qkv.rearrange("(p j) n -> p j n", j=PACK),
+        )
+        load_x(1)
+        angles = keep.tile([P, POS_PER_PART, HEAD_DIM], BF16)
+        nc.sync.dma_start(out=angles[:], in_=angle_rows)
+        for g in range(2, N_GROUPS):
+            load_x(g)
+
+        ident = keep.tile([P, P], F32)
+        make_identity(nc, ident[:])
+        minus_half = keep.tile([P, 2 * GROUP], F32)
+        nc.gpsimd.memset(minus_half[:], -0.5)
+        mean_sq = keep.tile([P, N_GROUPS * GROUP], F32)
+        floored = keep.tile([P, N_GROUPS * GROUP], F32)
+        rinv = keep.tile([P, N_GROUPS * GROUP], F32)
+        ones = keep.tile([P, P], BF16)
+        nc.vector.memset(ones[:], 1.0)
+        gamma_all = psum_keep.tile([P, DIM], F32)
+        nc.tensor.matmul(out=gamma_all[:], lhsT=ones[:], rhs=gamma_row[:], start=True, stop=True)
+
+        w_grouped = keep.tile([P, ROT_COLS + INNER, PACK], BF16, align_bytes=64)
+        nc.vector.tensor_copy(
+            out=w_grouped[:, 0 : 2 * INNER, :], in_=w_raw[:, :, 0 : 2 * INNER].rearrange("p j n -> p n j")
+        )
+        swapped = w_grouped[:, 2 * INNER : ROT_COLS, :].rearrange("p (g f i) j -> p g f i j", f=2, i=HALF)
+        plain = w_raw[:, :, 0 : 2 * INNER].rearrange("p j (g f i) -> p g f i j", f=2, i=HALF)
+        for f in range(2):
+            nc.vector.tensor_copy(out=swapped[:, :, f, :, :], in_=plain[:, :, 1 - f, :, :])
+        nc.vector.tensor_copy(
+            out=w_grouped[:, ROT_COLS:, :], in_=w_raw[:, :, 2 * INNER :].rearrange("p j n -> p n j")
+        )
+        w_codes = keep.tile([P, ROT_COLS + INNER], U32, align_bytes=64)
+        w_scales = keep.tile([P, ROT_COLS + INNER], U8, align_bytes=64)
+        nc.vector.quantize_mx(
+            out=w_codes[:, 0:ROT_COLS].bitcast(FP8X4),
+            scales=w_scales[:, 0:ROT_COLS],
+            in_=w_grouped[:, 0:ROT_COLS, :].rearrange("p n j -> p (n j)"),
+        )
+        nc.vector.quantize_mx(
+            out=w_codes[:, ROT_COLS:].bitcast(FP8X4),
+            scales=w_scales[:, ROT_COLS:],
+            in_=w_grouped[:, ROT_COLS:, :].rearrange("p n j -> p (n j)"),
+        )
+
+        table = keep.tile([P, POS_PER_PART, 2, 2, HEAD_DIM], F32)
+
+        grouped_of = {}
+        operand_of = {}
+        banks_of = {}
+        v_bank_of = {}
+        transposed_of = {}
+        products_of = {}
+
+        def sums(g):
+            b, t0 = where(g)
+            for i in range(GROUP):
+                junk = small.tile([P, DIM], BF16)
+                nc.scalar.activation(
+                    out=junk[:],
+                    in_=x_all[:, b, t0 + i, :],
+                    func=ACT.Square,
+                    scale=1.0 / math.sqrt(DIM),
+                    accum_out=mean_sq[:, g * GROUP + i : g * GROUP + i + 1],
+                )
+            if g == 0 or g % 2 == 1:
+                first = g if g < 2 else g - 1
+                cols = slice(first * GROUP, (g + 1) * GROUP)
+                nc.gpsimd.tensor_scalar_max(out=floored[:, cols], in0=mean_sq[:, cols], scalar1=EPS * EPS / DIM)
+                nc.gpsimd.tensor_tensor(
+                    out=rinv[:, cols],
+                    in0=floored[:, cols],
+                    in1=minus_half[:, 0 : (g + 1 - first) * GROUP],
+                    op=ALU.pow,
+                )
+
+        def fill_table(g):
+            b, t0 = where(g)
+            if b > 0:
+                return
+            ts = slice(t0, t0 + GROUP)
+            half_sin = small.tile([P, GROUP, HEAD_DIM], F32)
+            nc.scalar.activation(out=half_sin[:], in_=angles[:, ts, :], func=ACT.Sin, scale=0.5)
+            nc.scalar.activation(
+                out=table[:, ts, 1, 1, 0:HALF], in_=angles[:, ts, 0:HALF], func=ACT.Sin, scale=-1.0
+            )
+            twice_sq = small.tile([P, GROUP, HEAD_DIM], F32)
+            nc.scalar.activation(out=twice_sq[:], in_=half_sin[:], func=ACT.Square, scale=math.sqrt(2.0))
+            nc.scalar.activation(out=table[:, ts, 1, 1, HALF:], in_=angles[:, ts, HALF:], func=ACT.Sin)
+            nc.scalar.activation(out=table[:, ts, 0, 1, :], in_=twice_sq[:], func=ACT.Copy, scale=-1.0, bias=1.0)
+            nc.gpsimd.tensor_scalar(
+                out=table[:, ts, :, 0, :],
+                in0=table[:, ts, :, 1, :],
+                scalar1=math.sqrt(HEAD_DIM),
+                scalar2=0.0,
+                op0=ALU.mult,
+                op1=ALU.add,
+            )
+
+        def normalise(g):
+            b, t0 = where(g)
+            xn = work.tile([P, GROUP, DIM], BF16)
+            for i in range(GROUP):
+                nc.vector.scalar_tensor_tensor(
+                    out=xn[:, i, :],
+                    in0=x_all[:, b, t0 + i, :],
+                    scalar=rinv[:, g * GROUP + i : g * GROUP + i + 1],
+                    in1=gamma_all[:],
+                    op0=ALU.mult,
+                    op1=ALU.mult,
+                )
+            xn_words = xn[:].bitcast(F32)
+            pairs = []
+            for h in range(GROUP // 2):
+                xt = psum_t.tile([P, 2, 2, P], F32)
+                for i in range(2):
+                    for u in range(2):
+                        nc.tensor.transpose(xt[:, i, u, :], xn_words[:, 2 * h + i, u : 2 * P : 2], ident[:])
+                pairs.append(xt)
+            transposed_of[g] = pairs
+
+        def regroup(g):
+            pairs = transposed_of.pop(g)
+            grouped = work.tile([P, GROUP, P, PACK], BF16, align_bytes=64)
+            grouped_words = grouped[:].bitcast(F32)
+            for h in range(GROUP // 2):
+                nc.scalar.copy(
+                    out=grouped_words[:, 2 * h : 2 * h + 2, :, :], in_=pairs[h][:].rearrange("p i u r -> p i r u")
+                )
+            grouped_of[g] = grouped
+
+        def quantise(g):
+            grouped = grouped_of.pop(g)
+            codes = work.tile([P, GROUP * P], U32, align_bytes=64)
+            scales = work.tile([P, GROUP * P], U8, align_bytes=64)
+            nc.vector.quantize_mx(
+                out=codes[:].bitcast(FP8X4), scales=scales[:], in_=grouped[:].rearrange("p i r j -> p (i r j)")
+            )
+            operand_of[g] = (codes, scales)
+
+        def project(g):
+            codes, scales = operand_of.pop(g)
+            v_bank = psum_v.tile([P, GROUP, INNER], F32)
+            rot_banks = []
+            for i in range(GROUP):
+                rows = slice(i * P, (i + 1) * P)
+                rot_bank = psum_rot.tile([P, ROT_COLS], F32)
+                nc.tensor.matmul_mx(
+                    out=rot_bank[:],
+                    lhsT=codes[:, rows].bitcast(FP8X4),
+                    lhsT_scale=scales[:, rows],
+                    rhs=w_codes[:, 0:ROT_COLS].bitcast(FP8X4),
+                    rhs_scale=w_scales[:, 0:ROT_COLS],
+                    start=True,
+                    stop=True,
+                )
+                nc.tensor.matmul_mx(
+                    out=v_bank[:, i, :],
+                    lhsT=codes[:, rows].bitcast(FP8X4),
+                    lhsT_scale=scales[:, rows],
+                    rhs=w_codes[:, ROT_COLS:].bitcast(FP8X4),
+                    rhs_scale=w_scales[:, ROT_COLS:],
+                    start=True,
+                    stop=True,
+                )
+                rot_banks.append(rot_bank)
+            banks_of[g] = rot_banks
+            v_bank_of[g] = v_bank
+
+        def copy_v(g):
+            b, t0 = where(g)
+            v_bank = v_bank_of.pop(g)
+            v_out = results.tile([P, HEADS, GROUP, HEAD_DIM], F32)
+            nc.scalar.copy(
+                out=v_out[:].rearrange("p h i d -> p i h d"),
+                in_=v_bank[:].rearrange("p i (h d) -> p i h d", h=HEADS),
+            )
+            nc.sync.dma_start(out=v_rows[b, :, :, t0 : t0 + GROUP, :], in_=v_out[:])
+
+        def rotate(g):
+            b, t0 = where(g)
+            rot_banks = banks_of.pop(g)
+            products = results.tile([P, GROUP, ROT_COLS], F32)
+            for i in range(GROUP):
+                factors = table[:, t0 + i, :, :, :].rearrange("p c q d -> p (c q) d").unsqueeze(2)
+                nc.vector.tensor_tensor(
+                    out=products[:, i, :].rearrange("p (c h d) -> p c h d", h=HEADS, d=HEAD_DIM),
+                    in0=rot_banks[i][:].rearrange("p (c h d) -> p c h d", h=HEADS, d=HEAD_DIM),
+                    in1=factors.to_broadcast([P, 4, HEADS, HEAD_DIM]),
+                    op=ALU.mult,
+                )
+            products_of[g] = products
+
+        def add_and_store(g):
+            b, t0 = where(g)
+            products = products_of.pop(g)
+            qk_out = results.tile([P, 2 * HEADS, GROUP, HEAD_DIM], F32)
+            adder = nc.vector if g == N_GROUPS - 1 else nc.gpsimd
+            adder.tensor_tensor(
+                out=qk_out[:].rearrange("p g i d -> p i g d"),
+                in0=products[:, :, 0 : 2 * INNER].rearrange("p i (g d) -> p i g d", d=HEAD_DIM),
+                in1=products[:, :, 2 * INNER :].rearrange("p i (g d) -> p i g d", d=HEAD_DIM),
+                op=ALU.add,
+            )
+            nc.sync.dma_start(out=q_rows[b, :, :, t0 : t0 + GROUP, :], in_=qk_out[:, 0:HEADS, :, :])
+            nc.sync.dma_start(out=k_rows[b, :, :, t0 : t0 + GROUP, :], in_=qk_out[:, HEADS:, :, :])
+
+        def run(stage, g):
+            if 0 <= g < N_GROUPS:
+                stage(g)
+
+        for g in range(-5, N_GROUPS + 1):
+            run(project, g)
+            run(normalise, g + 2)
+            run(add_and_store, g - 1)
+            run(sums, g + 5)
+            run(copy_v, g)
+            run(regroup, g + 2)
+            run(fill_table, g + 2)
+            run(rotate, g)
+            run(quantise, g + 1)

@@ -6,6 +6,7 @@ from concourse.masks import make_identity
 
 F32 = mybir.dt.float32
 BF16 = mybir.dt.bfloat16
+I32 = mybir.dt.int32
 U32 = mybir.dt.uint32
 U8 = mybir.dt.uint8
 FP8X4 = mybir.dt.float8_e4m3fn_x4
@@ -17,13 +18,18 @@ BATCH, SEQ, DIM = 2, 4096, 512
 HEADS, HEAD_DIM = 2, 64
 HALF = HEAD_DIM // 2
 INNER = HEADS * HEAD_DIM
+ROT_COLS = 2 * INNER
+SECTIONS = ROT_COLS // HEAD_DIM
 PACK = 4
 POS_PER_PART = SEQ // P
+TILES = BATCH * POS_PER_PART
+PAIR = 2
 GROUP = 4
-GROUPS_PER_BATCH = POS_PER_PART // GROUP
-N_GROUPS = BATCH * GROUPS_PER_BATCH
-ROT_COLS = 4 * INNER
-EPS = 1e-12
+GROUP_SIZES = [PAIR, PAIR] + [GROUP] * (TILES // GROUP - 2) + [PAIR, PAIR]
+N_GROUPS = len(GROUP_SIZES)
+EARLY_TILES = 16
+TABLE_CHUNK = 8
+FLOOR = 1e-12 * 1e-12 / DIM
 
 FLOPS = 2 * BATCH * SEQ * DIM * 3 * INNER
 
@@ -38,8 +44,8 @@ def tile_ringattention_pa_t_kernel(tc, x, rotary_emb, gamma, w_qkv, out_0, out_1
 
     with ExitStack() as stack:
         keep = stack.enter_context(tc.tile_pool(name="keep", bufs=1))
-        small = stack.enter_context(tc.tile_pool(name="small", bufs=6))
-        work = stack.enter_context(tc.tile_pool(name="work", bufs=2))
+        small = stack.enter_context(tc.tile_pool(name="small", bufs=4))
+        work = stack.enter_context(tc.tile_pool(name="work", bufs=3))
         results = stack.enter_context(tc.tile_pool(name="results", bufs=3))
         psum_keep = stack.enter_context(tc.psum_pool(name="psum_keep", bufs=1))
         psum_t = stack.enter_context(tc.psum_pool(name="psum_t", bufs=2))
@@ -47,113 +53,83 @@ def tile_ringattention_pa_t_kernel(tc, x, rotary_emb, gamma, w_qkv, out_0, out_1
         psum_v = stack.enter_context(tc.psum_pool(name="psum_v", bufs=1))
         stack.enter_context(tc.manual_schedule())
 
-        def where(g):
-            c, b = divmod(g, BATCH)
-            return b, c * GROUP
+        def where(n):
+            c, b = divmod(n // GROUP, BATCH)
+            return b, c * GROUP + n % GROUP
+
+        def tiles_of(g):
+            n0 = sum(GROUP_SIZES[:g])
+            return n0, GROUP_SIZES[g]
 
         x_all = keep.tile([P, BATCH, POS_PER_PART, DIM], BF16)
 
-        def load_x(g):
-            b, t0 = where(g)
-            for t in range(t0, t0 + GROUP, 2):
-                nc.sync.dma_start(out=x_all[:, b, t : t + 2, :], in_=x_rows[b, :, t : t + 2, :])
+        def load_x(n):
+            b, t = where(n)
+            nc.sync.dma_start(out=x_all[:, b, t : t + PAIR, :], in_=x_rows[b, :, t : t + PAIR, :])
 
         load_x(0)
+        load_x(2)
         gamma_row = keep.tile([P, DIM], BF16)
         nc.vector.memset(gamma_row[:], 0.0)
         nc.sync.dma_start(out=gamma_row[0:1, :], in_=gamma.rearrange("(o k) -> o k", o=1))
+        load_x(4)
+        load_x(6)
         w_raw = keep.tile([P, PACK, 3 * INNER], BF16)
-        nc.sync.dma_start(
-            out=w_raw[:],
-            in_=w_qkv.rearrange("(p j) n -> p j n", j=PACK),
-        )
-        load_x(1)
+        nc.sync.dma_start(out=w_raw[:], in_=w_qkv.rearrange("(p j) n -> p j n", j=PACK))
+        for n in range(8, EARLY_TILES, PAIR):
+            load_x(n)
         angles = keep.tile([P, POS_PER_PART, HEAD_DIM], BF16)
         nc.sync.dma_start(out=angles[:], in_=angle_rows)
-        for g in range(2, N_GROUPS):
-            load_x(g)
+        for n in range(EARLY_TILES, TILES, PAIR):
+            load_x(n)
 
         ident = keep.tile([P, P], F32)
         make_identity(nc, ident[:])
-        minus_half = keep.tile([P, 2 * GROUP], F32)
-        nc.gpsimd.memset(minus_half[:], -0.5)
-        mean_sq = keep.tile([P, N_GROUPS * GROUP], F32)
-        floored = keep.tile([P, N_GROUPS * GROUP], F32)
-        rinv = keep.tile([P, N_GROUPS * GROUP], F32)
+        one = keep.tile([P, 1], F32)
+        nc.vector.memset(one[:], 1.0)
+        nc.scalar.activation(out=one[:], in_=one[:], func=ACT.Sqrt)
+        mean_sq = keep.tile([P, TILES], F32)
+        above = keep.tile([P, TILES], F32)
+        rms = keep.tile([P, TILES], F32)
+        rinv = keep.tile([P, TILES], F32)
         ones = keep.tile([P, P], BF16)
         nc.vector.memset(ones[:], 1.0)
         gamma_all = psum_keep.tile([P, DIM], F32)
         nc.tensor.matmul(out=gamma_all[:], lhsT=ones[:], rhs=gamma_row[:], start=True, stop=True)
 
-        w_grouped = keep.tile([P, ROT_COLS + INNER, PACK], BF16, align_bytes=64)
-        nc.vector.tensor_copy(
-            out=w_grouped[:, 0 : 2 * INNER, :], in_=w_raw[:, :, 0 : 2 * INNER].rearrange("p j n -> p n j")
-        )
-        swapped = w_grouped[:, 2 * INNER : ROT_COLS, :].rearrange("p (g f i) j -> p g f i j", f=2, i=HALF)
-        plain = w_raw[:, :, 0 : 2 * INNER].rearrange("p j (g f i) -> p g f i j", f=2, i=HALF)
-        for f in range(2):
-            nc.vector.tensor_copy(out=swapped[:, :, f, :, :], in_=plain[:, :, 1 - f, :, :])
-        nc.vector.tensor_copy(
-            out=w_grouped[:, ROT_COLS:, :], in_=w_raw[:, :, 2 * INNER :].rearrange("p j n -> p n j")
-        )
         w_codes = keep.tile([P, ROT_COLS + INNER], U32, align_bytes=64)
         w_scales = keep.tile([P, ROT_COLS + INNER], U8, align_bytes=64)
-        nc.vector.quantize_mx(
-            out=w_codes[:, 0:ROT_COLS].bitcast(FP8X4),
-            scales=w_scales[:, 0:ROT_COLS],
-            in_=w_grouped[:, 0:ROT_COLS, :].rearrange("p n j -> p (n j)"),
-        )
-        nc.vector.quantize_mx(
-            out=w_codes[:, ROT_COLS:].bitcast(FP8X4),
-            scales=w_scales[:, ROT_COLS:],
-            in_=w_grouped[:, ROT_COLS:, :].rearrange("p n j -> p (n j)"),
-        )
-
+        magnitudes = keep.tile([P, POS_PER_PART, HEAD_DIM], BF16)
         table = keep.tile([P, POS_PER_PART, 2, 2, HEAD_DIM], F32)
 
-        grouped_of = {}
-        operand_of = {}
-        banks_of = {}
-        v_bank_of = {}
-        transposed_of = {}
-        products_of = {}
-
-        def sums(g):
-            b, t0 = where(g)
-            for i in range(GROUP):
-                junk = small.tile([P, DIM], BF16)
-                nc.scalar.activation(
-                    out=junk[:],
-                    in_=x_all[:, b, t0 + i, :],
-                    func=ACT.Square,
-                    scale=1.0 / math.sqrt(DIM),
-                    accum_out=mean_sq[:, g * GROUP + i : g * GROUP + i + 1],
-                )
-            if g == 0 or g % 2 == 1:
-                first = g if g < 2 else g - 1
-                cols = slice(first * GROUP, (g + 1) * GROUP)
-                nc.gpsimd.tensor_scalar_max(out=floored[:, cols], in0=mean_sq[:, cols], scalar1=EPS * EPS / DIM)
-                nc.gpsimd.tensor_tensor(
-                    out=rinv[:, cols],
-                    in0=floored[:, cols],
-                    in1=minus_half[:, 0 : (g + 1 - first) * GROUP],
-                    op=ALU.pow,
+        def prepare_weights():
+            w_grouped = keep.tile([P, ROT_COLS + INNER, PACK], BF16, align_bytes=64)
+            nc.vector.tensor_copy(out=w_grouped[:], in_=w_raw[:].rearrange("p j n -> p n j"))
+            for cols in (slice(0, ROT_COLS), slice(ROT_COLS, ROT_COLS + INNER)):
+                nc.vector.quantize_mx(
+                    out=w_codes[:, cols].bitcast(FP8X4),
+                    scales=w_scales[:, cols],
+                    in_=w_grouped[:, cols, :].rearrange("p n j -> p (n j)"),
                 )
 
-        def fill_table(g):
-            b, t0 = where(g)
-            if b > 0:
-                return
-            ts = slice(t0, t0 + GROUP)
-            half_sin = small.tile([P, GROUP, HEAD_DIM], F32)
-            nc.scalar.activation(out=half_sin[:], in_=angles[:, ts, :], func=ACT.Sin, scale=0.5)
-            nc.scalar.activation(
-                out=table[:, ts, 1, 1, 0:HALF], in_=angles[:, ts, 0:HALF], func=ACT.Sin, scale=-1.0
+        def take_magnitudes():
+            nc.vector.tensor_scalar(
+                out=magnitudes[:].rearrange("p t d -> p (t d)").bitcast(I32),
+                in0=angles[:].rearrange("p t d -> p (t d)").bitcast(I32),
+                scalar1=0x7FFF7FFF,
+                scalar2=None,
+                op0=ALU.bitwise_and,
             )
-            twice_sq = small.tile([P, GROUP, HEAD_DIM], F32)
-            nc.scalar.activation(out=twice_sq[:], in_=half_sin[:], func=ACT.Square, scale=math.sqrt(2.0))
-            nc.scalar.activation(out=table[:, ts, 1, 1, HALF:], in_=angles[:, ts, HALF:], func=ACT.Sin)
-            nc.scalar.activation(out=table[:, ts, 0, 1, :], in_=twice_sq[:], func=ACT.Copy, scale=-1.0, bias=1.0)
+
+        def fill_table(t0):
+            ts = slice(t0, t0 + TABLE_CHUNK)
+            nc.scalar.activation(
+                out=table[:, ts, 0, 1, :], in_=magnitudes[:, ts, :], func=ACT.Sin, scale=-1.0, bias=math.pi / 2
+            )
+            nc.scalar.activation(out=table[:, ts, 1, 1, 0:HALF], in_=angles[:, ts, HALF:], func=ACT.Sin)
+            nc.scalar.activation(
+                out=table[:, ts, 1, 1, HALF:], in_=angles[:, ts, 0:HALF], func=ACT.Sin, scale=-1.0
+            )
             nc.gpsimd.tensor_scalar(
                 out=table[:, ts, :, 0, :],
                 in0=table[:, ts, :, 1, :],
@@ -163,125 +139,204 @@ def tile_ringattention_pa_t_kernel(tc, x, rotary_emb, gamma, w_qkv, out_0, out_1
                 op1=ALU.add,
             )
 
-        def normalise(g):
-            b, t0 = where(g)
-            xn = work.tile([P, GROUP, DIM], BF16)
-            for i in range(GROUP):
-                nc.vector.scalar_tensor_tensor(
-                    out=xn[:, i, :],
-                    in0=x_all[:, b, t0 + i, :],
-                    scalar=rinv[:, g * GROUP + i : g * GROUP + i + 1],
-                    in1=gamma_all[:],
-                    op0=ALU.mult,
-                    op1=ALU.mult,
-                )
-            xn_words = xn[:].bitcast(F32)
-            pairs = []
-            for h in range(GROUP // 2):
-                xt = psum_t.tile([P, 2, 2, P], F32)
-                for i in range(2):
-                    for u in range(2):
-                        nc.tensor.transpose(xt[:, i, u, :], xn_words[:, 2 * h + i, u : 2 * P : 2], ident[:])
-                pairs.append(xt)
-            transposed_of[g] = pairs
+        transposed_of, grouped_of, operand_of = {}, {}, {}
+        banks_of, v_bank_of, products_of = {}, {}, {}
 
-        def regroup(g):
-            pairs = transposed_of.pop(g)
-            grouped = work.tile([P, GROUP, P, PACK], BF16, align_bytes=64)
-            grouped_words = grouped[:].bitcast(F32)
-            for h in range(GROUP // 2):
+        def scalar_sum(n):
+            b, t = where(n)
+            junk = small.tile([P, DIM], BF16)
+            nc.scalar.activation(
+                out=junk[:],
+                in_=x_all[:, b, t, :],
+                func=ACT.Square,
+                scale=1.0 / math.sqrt(DIM),
+                accum_out=mean_sq[:, n : n + 1],
+            )
+
+        def vector_sum(n):
+            b, t = where(n)
+            squares = small.tile([P, DIM], BF16)
+            nc.vector.scalar_tensor_tensor(
+                out=squares[:],
+                in0=x_all[:, b, t, :],
+                scalar=1.0 / DIM,
+                in1=x_all[:, b, t, :],
+                op0=ALU.mult,
+                op1=ALU.mult,
+                accum_out=mean_sq[:, n : n + 1],
+            )
+
+        def root(n0, tiles):
+            cols = slice(n0, n0 + tiles)
+            nc.scalar.activation(out=above[:, cols], in_=mean_sq[:, cols], func=ACT.Relu, bias=-FLOOR)
+            nc.scalar.activation(out=rms[:, cols], in_=above[:, cols], func=ACT.Sqrt, bias=FLOOR)
+
+        def invert(n0, tiles):
+            cols = slice(n0, n0 + tiles)
+            nc.vector.reciprocal(out=rinv[:, cols], in_=rms[:, cols])
+
+        def normalise(g):
+            n0, tiles = tiles_of(g)
+            transposed_of[g] = []
+            for h in range(tiles // PAIR):
+                xn = work.tile([P, PAIR, DIM], BF16)
+                transposed = psum_t.tile([P, PAIR, 2, P], F32)
+                for i in range(PAIR):
+                    n = n0 + h * PAIR + i
+                    b, t = where(n)
+                    nc.vector.scalar_tensor_tensor(
+                        out=xn[:, i, :],
+                        in0=x_all[:, b, t, :],
+                        scalar=rinv[:, n : n + 1],
+                        in1=gamma_all[:],
+                        op0=ALU.mult,
+                        op1=ALU.mult,
+                    )
+                xn_words = xn[:].bitcast(F32)
+                for i in range(PAIR):
+                    for u in range(2):
+                        nc.tensor.transpose(transposed[:, i, u, :], xn_words[:, i, u : 2 * P : 2], ident[:])
+                transposed_of[g].append(transposed)
+
+        def regroup(g, h):
+            n0, tiles = tiles_of(g)
+            if h == 0:
+                grouped_new = work.tile([P, GROUP, P, PACK], BF16, align_bytes=64)
+                grouped_of[g] = grouped_new
+            if h < tiles // PAIR:
                 nc.scalar.copy(
-                    out=grouped_words[:, 2 * h : 2 * h + 2, :, :], in_=pairs[h][:].rearrange("p i u r -> p i r u")
+                    out=grouped_of[g][:].bitcast(F32)[:, h * PAIR : (h + 1) * PAIR, :, :],
+                    in_=transposed_of[g][h][:].rearrange("p i u r -> p i r u"),
                 )
-            grouped_of[g] = grouped
 
         def quantise(g):
-            grouped = grouped_of.pop(g)
+            n0, tiles = tiles_of(g)
             codes = work.tile([P, GROUP * P], U32, align_bytes=64)
             scales = work.tile([P, GROUP * P], U8, align_bytes=64)
             nc.vector.quantize_mx(
-                out=codes[:].bitcast(FP8X4), scales=scales[:], in_=grouped[:].rearrange("p i r j -> p (i r j)")
+                out=codes[:, 0 : tiles * P].bitcast(FP8X4),
+                scales=scales[:, 0 : tiles * P],
+                in_=grouped_of.pop(g)[:, 0:tiles, :, :].rearrange("p i r j -> p (i r j)"),
             )
             operand_of[g] = (codes, scales)
 
         def project(g):
+            n0, tiles = tiles_of(g)
             codes, scales = operand_of.pop(g)
             v_bank = psum_v.tile([P, GROUP, INNER], F32)
-            rot_banks = []
-            for i in range(GROUP):
+            banks_of[g] = []
+            for i in range(tiles):
                 rows = slice(i * P, (i + 1) * P)
-                rot_bank = psum_rot.tile([P, ROT_COLS], F32)
-                nc.tensor.matmul_mx(
-                    out=rot_bank[:],
-                    lhsT=codes[:, rows].bitcast(FP8X4),
-                    lhsT_scale=scales[:, rows],
-                    rhs=w_codes[:, 0:ROT_COLS].bitcast(FP8X4),
-                    rhs_scale=w_scales[:, 0:ROT_COLS],
-                    start=True,
-                    stop=True,
-                )
-                nc.tensor.matmul_mx(
-                    out=v_bank[:, i, :],
-                    lhsT=codes[:, rows].bitcast(FP8X4),
-                    lhsT_scale=scales[:, rows],
-                    rhs=w_codes[:, ROT_COLS:].bitcast(FP8X4),
-                    rhs_scale=w_scales[:, ROT_COLS:],
-                    start=True,
-                    stop=True,
-                )
-                rot_banks.append(rot_bank)
-            banks_of[g] = rot_banks
+                if i % PAIR == 0:
+                    bank = psum_rot.tile([P, PAIR, ROT_COLS], F32)
+                    banks_of[g].append(bank)
+                for out, cols in (
+                    (bank[:, i % PAIR, :], slice(0, ROT_COLS)),
+                    (v_bank[:, i, :], slice(ROT_COLS, ROT_COLS + INNER)),
+                ):
+                    nc.tensor.matmul_mx(
+                        out=out,
+                        lhsT=codes[:, rows].bitcast(FP8X4),
+                        lhsT_scale=scales[:, rows],
+                        rhs=w_codes[:, cols].bitcast(FP8X4),
+                        rhs_scale=w_scales[:, cols],
+                        start=True,
+                        stop=True,
+                    )
             v_bank_of[g] = v_bank
 
-        def copy_v(g):
-            b, t0 = where(g)
-            v_bank = v_bank_of.pop(g)
+        def shared(g):
+            return tiles_of(g)[1] == GROUP and g < N_GROUPS - 5
+
+        def multiply(engine, g, i, tiles, rot):
+            b, t = where(tiles_of(g)[0])
+            shape = [P, tiles, 2, 2, HEADS, HEAD_DIM]
+            engine.tensor_tensor(
+                out=products_of[g][:, :, i : i + tiles, :].rearrange("p c i (q h d) -> p i c q h d", q=2, h=HEADS),
+                in0=rot.rearrange("p i (q h d) -> p i q h d", q=2, h=HEADS).unsqueeze(2).to_broadcast(shape),
+                in1=table[:, t + i : t + i + tiles, :, :, :].unsqueeze(4).to_broadcast(shape),
+                op=ALU.mult,
+            )
+
+        def copy_out(g):
+            n0, tiles = tiles_of(g)
+            b, t = where(n0)
+            products = results.tile([P, 2, GROUP, ROT_COLS], F32)
+            products_of[g] = products
+            if shared(g):
+                copied = work.tile([P, 1, ROT_COLS], F32)
+                nc.scalar.copy(out=copied[:], in_=banks_of[g][1][:, 1:2, :])
+                multiply(nc.gpsimd, g, GROUP - 1, 1, copied[:])
             v_out = results.tile([P, HEADS, GROUP, HEAD_DIM], F32)
             nc.scalar.copy(
-                out=v_out[:].rearrange("p h i d -> p i h d"),
-                in_=v_bank[:].rearrange("p i (h d) -> p i h d", h=HEADS),
+                out=v_out[:, :, 0:tiles, :].rearrange("p h i d -> p i h d"),
+                in_=v_bank_of.pop(g)[:, 0:tiles, :].rearrange("p i (h d) -> p i h d", h=HEADS),
             )
-            nc.sync.dma_start(out=v_rows[b, :, :, t0 : t0 + GROUP, :], in_=v_out[:])
+            nc.sync.dma_start(out=v_rows[b, :, :, t : t + tiles, :], in_=v_out[:, :, 0:tiles, :])
 
         def rotate(g):
-            b, t0 = where(g)
-            rot_banks = banks_of.pop(g)
-            products = results.tile([P, GROUP, ROT_COLS], F32)
-            for i in range(GROUP):
-                factors = table[:, t0 + i, :, :, :].rearrange("p c q d -> p (c q) d").unsqueeze(2)
-                nc.vector.tensor_tensor(
-                    out=products[:, i, :].rearrange("p (c h d) -> p c h d", h=HEADS, d=HEAD_DIM),
-                    in0=rot_banks[i][:].rearrange("p (c h d) -> p c h d", h=HEADS, d=HEAD_DIM),
-                    in1=factors.to_broadcast([P, 4, HEADS, HEAD_DIM]),
-                    op=ALU.mult,
-                )
-            products_of[g] = products
+            for h, bank in enumerate(banks_of.pop(g)):
+                tiles = 1 if h == 1 and shared(g) else PAIR
+                multiply(nc.vector, g, h * PAIR, tiles, bank[:, 0:tiles, :])
 
         def add_and_store(g):
-            b, t0 = where(g)
+            n0, tiles = tiles_of(g)
+            b, t = where(n0)
             products = products_of.pop(g)
-            qk_out = results.tile([P, 2 * HEADS, GROUP, HEAD_DIM], F32)
+            qk_out = results.tile([P, SECTIONS, GROUP, HEAD_DIM], F32)
             adder = nc.vector if g == N_GROUPS - 1 else nc.gpsimd
+            halves = products[:].rearrange("p c i (g f e) -> p c i g f e", g=SECTIONS, f=2)
             adder.tensor_tensor(
-                out=qk_out[:].rearrange("p g i d -> p i g d"),
-                in0=products[:, :, 0 : 2 * INNER].rearrange("p i (g d) -> p i g d", d=HEAD_DIM),
-                in1=products[:, :, 2 * INNER :].rearrange("p i (g d) -> p i g d", d=HEAD_DIM),
+                out=qk_out[:, :, 0:tiles, :].rearrange("p g i (f e) -> p i g f e", f=2),
+                in0=halves[:, 0, 0:tiles, :, :, :],
+                in1=halves[:, 1, 0:tiles, :, ::-1, :],
                 op=ALU.add,
             )
-            nc.sync.dma_start(out=q_rows[b, :, :, t0 : t0 + GROUP, :], in_=qk_out[:, 0:HEADS, :, :])
-            nc.sync.dma_start(out=k_rows[b, :, :, t0 : t0 + GROUP, :], in_=qk_out[:, HEADS:, :, :])
+            ts = slice(t, t + tiles)
+            nc.sync.dma_start(out=q_rows[b, :, :, ts, :], in_=qk_out[:, 0:HEADS, 0:tiles, :])
+            nc.sync.dma_start(out=k_rows[b, :, :, ts, :], in_=qk_out[:, HEADS:, 0:tiles, :])
 
-        def run(stage, g):
+        for n in range(EARLY_TILES):
+            if n % 2 == 1 and n < 12:
+                vector_sum(n)
+            else:
+                scalar_sum(n)
+            if n == 7:
+                root(0, 8)
+                pass
+        root(8, EARLY_TILES - 8)
+        prepare_weights()
+        take_magnitudes()
+        fill_table(0)
+        invert(0, 8)
+
+        def run(stage, g, *more):
             if 0 <= g < N_GROUPS:
-                stage(g)
+                stage(g, *more)
 
-        for g in range(-5, N_GROUPS + 1):
+        def squares(g, lo, hi):
+            if 5 <= g < N_GROUPS:
+                n0, tiles = tiles_of(g)
+                for n in range(n0 + lo, n0 + min(hi, tiles)):
+                    scalar_sum(n)
+
+        for g in range(-2, N_GROUPS + 1):
+            run(quantise, g)
             run(project, g)
             run(normalise, g + 2)
             run(add_and_store, g - 1)
-            run(sums, g + 5)
-            run(copy_v, g)
-            run(regroup, g + 2)
-            run(fill_table, g + 2)
+            if g == -2:
+                invert(8, EARLY_TILES - 8)
+            squares(g + 5, 0, 2)
+            run(copy_out, g)
+            run(regroup, g + 2, 0)
+            squares(g + 5, 2, 4)
+            run(regroup, g + 2, 1)
+            if g == -1:
+                for t0 in range(TABLE_CHUNK, POS_PER_PART, TABLE_CHUNK):
+                    fill_table(t0)
+            if g >= 0 and g + 5 < N_GROUPS:
+                root(*tiles_of(g + 5))
+            if g >= 2 and g + 5 - 2 < N_GROUPS:
+                invert(*tiles_of(g + 5 - 2))
             run(rotate, g)
-            run(quantise, g + 1)

@@ -49,8 +49,8 @@ def tile_ringattention_pa_t_kernel(tc, x, rotary_emb, gamma, w_qkv, out_0, out_1
         results = stack.enter_context(tc.tile_pool(name="results", bufs=3))
         psum_keep = stack.enter_context(tc.psum_pool(name="psum_keep", bufs=1))
         psum_t = stack.enter_context(tc.psum_pool(name="psum_t", bufs=2))
-        psum_rot = stack.enter_context(tc.psum_pool(name="psum_rot", bufs=4))
-        psum_v = stack.enter_context(tc.psum_pool(name="psum_v", bufs=1))
+        psum_rot = stack.enter_context(tc.psum_pool(name="psum_rot", bufs=3))
+        psum_v = stack.enter_context(tc.psum_pool(name="psum_v", bufs=2))
         stack.enter_context(tc.manual_schedule())
 
         def where(n):
@@ -74,10 +74,10 @@ def tile_ringattention_pa_t_kernel(tc, x, rotary_emb, gamma, w_qkv, out_0, out_1
         nc.sync.dma_start(out=gamma_row[0:1, :], in_=gamma.rearrange("(o k) -> o k", o=1))
         load_x(4)
         load_x(6)
-        w_raw = keep.tile([P, PACK, 3 * INNER], BF16)
-        nc.sync.dma_start(out=w_raw[:], in_=w_qkv.rearrange("(p j) n -> p j n", j=PACK))
         for n in range(8, EARLY_TILES, PAIR):
             load_x(n)
+        w_raw = keep.tile([P, PACK, 3 * INNER], BF16)
+        nc.sync.dma_start(out=w_raw[:], in_=w_qkv.rearrange("(p j) n -> p j n", j=PACK))
         angles = keep.tile([P, POS_PER_PART, HEAD_DIM], BF16)
         nc.sync.dma_start(out=angles[:], in_=angle_rows)
         for n in range(EARLY_TILES, TILES, PAIR):
@@ -102,9 +102,19 @@ def tile_ringattention_pa_t_kernel(tc, x, rotary_emb, gamma, w_qkv, out_0, out_1
         magnitudes = keep.tile([P, POS_PER_PART, HEAD_DIM], BF16)
         table = keep.tile([P, POS_PER_PART, 2, 2, HEAD_DIM], F32)
 
-        def prepare_weights():
-            w_grouped = keep.tile([P, ROT_COLS + INNER, PACK], BF16, align_bytes=64)
-            nc.vector.tensor_copy(out=w_grouped[:], in_=w_raw[:].rearrange("p j n -> p n j"))
+        w_grouped = keep.tile([P, ROT_COLS + INNER, PACK], BF16, align_bytes=64)
+
+        def group_weights():
+            nc.gpsimd.tensor_scalar(
+                out=w_grouped[:],
+                in0=w_raw[:].rearrange("p j n -> p n j"),
+                scalar1=1.0,
+                scalar2=0.0,
+                op0=ALU.mult,
+                op1=ALU.add,
+            )
+
+        def quantise_weights():
             for cols in (slice(0, ROT_COLS), slice(ROT_COLS, ROT_COLS + INNER)):
                 nc.vector.quantize_mx(
                     out=w_codes[:, cols].bitcast(FP8X4),
@@ -179,7 +189,7 @@ def tile_ringattention_pa_t_kernel(tc, x, rotary_emb, gamma, w_qkv, out_0, out_1
             n0, tiles = tiles_of(g)
             transposed_of[g] = []
             for h in range(tiles // PAIR):
-                xn = work.tile([P, PAIR, DIM], BF16)
+                xn = work.tile([P, PAIR, DIM], BF16, bufs=6)
                 transposed = psum_t.tile([P, PAIR, 2, P], F32)
                 for i in range(PAIR):
                     n = n0 + h * PAIR + i
@@ -198,13 +208,13 @@ def tile_ringattention_pa_t_kernel(tc, x, rotary_emb, gamma, w_qkv, out_0, out_1
                         nc.tensor.transpose(transposed[:, i, u, :], xn_words[:, i, u : 2 * P : 2], ident[:])
                 transposed_of[g].append(transposed)
 
-        def regroup(g, h):
+        def regroup(g, h, copy=nc.scalar.copy):
             n0, tiles = tiles_of(g)
             if h == 0:
                 grouped_new = work.tile([P, GROUP, P, PACK], BF16, align_bytes=64)
                 grouped_of[g] = grouped_new
             if h < tiles // PAIR:
-                nc.scalar.copy(
+                copy(
                     out=grouped_of[g][:].bitcast(F32)[:, h * PAIR : (h + 1) * PAIR, :, :],
                     in_=transposed_of[g][h][:].rearrange("p i u r -> p i r u"),
                 )
@@ -246,7 +256,7 @@ def tile_ringattention_pa_t_kernel(tc, x, rotary_emb, gamma, w_qkv, out_0, out_1
             v_bank_of[g] = v_bank
 
         def shared(g):
-            return tiles_of(g)[1] == GROUP and g < N_GROUPS - 5
+            return tiles_of(g)[1] == GROUP and 2 < g < N_GROUPS - 4
 
         def multiply(engine, g, i, tiles, rot):
             b, t = where(tiles_of(g)[0])
@@ -296,6 +306,12 @@ def tile_ringattention_pa_t_kernel(tc, x, rotary_emb, gamma, w_qkv, out_0, out_1
             nc.sync.dma_start(out=q_rows[b, :, :, ts, :], in_=qk_out[:, 0:HEADS, 0:tiles, :])
             nc.sync.dma_start(out=k_rows[b, :, :, ts, :], in_=qk_out[:, HEADS:, 0:tiles, :])
 
+        def squares(g, lo, hi):
+            if g < N_GROUPS:
+                n0, tiles = tiles_of(g)
+                for n in range(n0 + lo, n0 + min(hi, tiles)):
+                    scalar_sum(n)
+
         for n in range(EARLY_TILES):
             if n % 2 == 1 and n < 12:
                 vector_sum(n)
@@ -303,40 +319,59 @@ def tile_ringattention_pa_t_kernel(tc, x, rotary_emb, gamma, w_qkv, out_0, out_1
                 scalar_sum(n)
             if n == 7:
                 root(0, 8)
-                pass
         root(8, EARLY_TILES - 8)
-        prepare_weights()
-        take_magnitudes()
-        fill_table(0)
+        group_weights()
         invert(0, 8)
+        normalise(0)
+        normalise(1)
+        regroup(0, 0)
+        regroup(1, 0)
+        quantise_weights()
+        take_magnitudes()
+        invert(8, EARLY_TILES - 8)
+        normalise(2)
+        fill_table(0)
+        quantise(0)
+        project(0)
+        quantise(1)
+        project(1)
+        regroup(2, 0)
+        regroup(2, 1)
+        normalise(3)
+        copy_out(0)
+        copy_out(1)
+        fill_table(8)
+        fill_table(16)
+        fill_table(24)
+        rotate(0)
+        regroup(3, 0, nc.vector.tensor_copy)
+        add_and_store(0)
+        rotate(1)
+        regroup(3, 1, nc.vector.tensor_copy)
 
-        def run(stage, g, *more):
-            if 0 <= g < N_GROUPS:
-                stage(g, *more)
-
-        def squares(g, lo, hi):
-            if 5 <= g < N_GROUPS:
-                n0, tiles = tiles_of(g)
-                for n in range(n0 + lo, n0 + min(hi, tiles)):
-                    scalar_sum(n)
-
-        for g in range(-2, N_GROUPS + 1):
-            run(quantise, g)
-            run(project, g)
-            run(normalise, g + 2)
-            run(add_and_store, g - 1)
-            if g == -2:
-                invert(8, EARLY_TILES - 8)
-            squares(g + 5, 0, 2)
-            run(copy_out, g)
-            run(regroup, g + 2, 0)
-            squares(g + 5, 2, 4)
-            run(regroup, g + 2, 1)
-            if g == -1:
-                for t0 in range(TABLE_CHUNK, POS_PER_PART, TABLE_CHUNK):
-                    fill_table(t0)
-            if g >= 0 and g + 5 < N_GROUPS:
-                root(*tiles_of(g + 5))
-            if g >= 2 and g + 5 - 2 < N_GROUPS:
-                invert(*tiles_of(g + 5 - 2))
-            run(rotate, g)
+        last = N_GROUPS - 1
+        for g in range(2, last):
+            quantise(g)
+            if g == last - 1:
+                quantise(last)
+            project(g)
+            if g == last - 1:
+                project(last)
+            if g + 2 < N_GROUPS:
+                normalise(g + 2)
+            add_and_store(g - 1)
+            squares(g + 3, 0, 4)
+            if g + 3 < N_GROUPS:
+                root(*tiles_of(g + 3))
+            copy_out(g)
+            if g + 2 < N_GROUPS:
+                regroup(g + 2, 0)
+            if g + 2 < N_GROUPS:
+                regroup(g + 2, 1)
+            rotate(g)
+            if g + 3 < N_GROUPS:
+                invert(*tiles_of(g + 3))
+        add_and_store(last - 1)
+        copy_out(last)
+        rotate(last)
+        add_and_store(last)

@@ -176,10 +176,17 @@ def tile_ringattention_pa_t_kernel(tc, x, rotary_emb, gamma, w_qkv, out_0, out_1
                 accum_out=mean_sq[:, n : n + 1],
             )
 
-        def root(n0, tiles):
+        def floor_a(n0, tiles):
             cols = slice(n0, n0 + tiles)
             nc.scalar.activation(out=above[:, cols], in_=mean_sq[:, cols], func=ACT.Relu, bias=-FLOOR)
+
+        def root_b(n0, tiles):
+            cols = slice(n0, n0 + tiles)
             nc.scalar.activation(out=rms[:, cols], in_=above[:, cols], func=ACT.Sqrt, bias=FLOOR)
+
+        def root(n0, tiles):
+            floor_a(n0, tiles)
+            root_b(n0, tiles)
 
         def invert(n0, tiles):
             cols = slice(n0, n0 + tiles)
@@ -256,7 +263,7 @@ def tile_ringattention_pa_t_kernel(tc, x, rotary_emb, gamma, w_qkv, out_0, out_1
             v_bank_of[g] = v_bank
 
         def shared(g):
-            return tiles_of(g)[1] == GROUP and 2 < g < N_GROUPS - 4
+            return (1 if 2 < g < N_GROUPS - 4 else 0) if tiles_of(g)[1] == GROUP else 0
 
         def multiply(engine, g, i, tiles, rot):
             b, t = where(tiles_of(g)[0])
@@ -268,15 +275,18 @@ def tile_ringattention_pa_t_kernel(tc, x, rotary_emb, gamma, w_qkv, out_0, out_1
                 op=ALU.mult,
             )
 
-        def copy_out(g):
-            n0, tiles = tiles_of(g)
-            b, t = where(n0)
+        def copy_t(g):
             products = results.tile([P, 2, GROUP, ROT_COLS], F32)
             products_of[g] = products
             if shared(g):
-                copied = work.tile([P, 1, ROT_COLS], F32)
-                nc.scalar.copy(out=copied[:], in_=banks_of[g][1][:, 1:2, :])
-                multiply(nc.gpsimd, g, GROUP - 1, 1, copied[:])
+                n_s = shared(g)
+                copied = work.tile([P, PAIR, ROT_COLS], F32)
+                nc.scalar.copy(out=copied[:, 0:n_s, :], in_=banks_of[g][1][:, PAIR - n_s :, :])
+                multiply(nc.gpsimd, g, GROUP - n_s, n_s, copied[:, 0:n_s, :])
+
+        def copy_v(g):
+            n0, tiles = tiles_of(g)
+            b, t = where(n0)
             v_out = results.tile([P, HEADS, GROUP, HEAD_DIM], F32)
             nc.scalar.copy(
                 out=v_out[:, :, 0:tiles, :].rearrange("p h i d -> p i h d"),
@@ -284,10 +294,15 @@ def tile_ringattention_pa_t_kernel(tc, x, rotary_emb, gamma, w_qkv, out_0, out_1
             )
             nc.sync.dma_start(out=v_rows[b, :, :, t : t + tiles, :], in_=v_out[:, :, 0:tiles, :])
 
+        def copy_out(g):
+            copy_t(g)
+            copy_v(g)
+
         def rotate(g):
             for h, bank in enumerate(banks_of.pop(g)):
-                tiles = 1 if h == 1 and shared(g) else PAIR
-                multiply(nc.vector, g, h * PAIR, tiles, bank[:, 0:tiles, :])
+                tiles = PAIR - shared(g) if h == 1 else PAIR
+                if tiles > 0:
+                    multiply(nc.vector, g, h * PAIR, tiles, bank[:, 0:tiles, :])
 
         def add_and_store(g):
             n0, tiles = tiles_of(g)
@@ -361,9 +376,12 @@ def tile_ringattention_pa_t_kernel(tc, x, rotary_emb, gamma, w_qkv, out_0, out_1
                 normalise(g + 2)
             add_and_store(g - 1)
             squares(g + 3, 0, 4)
+            copy_t(g)
             if g + 3 < N_GROUPS:
-                root(*tiles_of(g + 3))
-            copy_out(g)
+                floor_a(*tiles_of(g + 3))
+            copy_v(g)
+            if g + 3 < N_GROUPS:
+                root_b(*tiles_of(g + 3))
             if g + 2 < N_GROUPS:
                 regroup(g + 2, 0)
             if g + 2 < N_GROUPS:

@@ -87,10 +87,9 @@ def tile_ringattention_pa_t_kernel(tc, x, rotary_emb, gamma, w_qkv, out_0, out_1
         make_identity(nc, ident[:])
         one = keep.tile([P, 1], F32)
         nc.vector.memset(one[:], 1.0)
-        nc.scalar.activation(out=one[:], in_=one[:], func=ACT.Sqrt)
+        nc.scalar.activation(out=one[:], in_=one[:], func=ACT.Abs_reciprocal_sqrt)
         mean_sq = keep.tile([P, TILES], F32)
         above = keep.tile([P, TILES], F32)
-        rms = keep.tile([P, TILES], F32)
         rinv = keep.tile([P, TILES], F32)
         ones = keep.tile([P, P], BF16)
         nc.vector.memset(ones[:], 1.0)
@@ -182,15 +181,13 @@ def tile_ringattention_pa_t_kernel(tc, x, rotary_emb, gamma, w_qkv, out_0, out_1
 
         def root_b(n0, tiles):
             cols = slice(n0, n0 + tiles)
-            nc.scalar.activation(out=rms[:, cols], in_=above[:, cols], func=ACT.Sqrt, bias=FLOOR)
+            nc.scalar.activation(
+                out=rinv[:, cols], in_=above[:, cols], func=ACT.Abs_reciprocal_sqrt, bias=FLOOR
+            )
 
         def root(n0, tiles):
             floor_a(n0, tiles)
             root_b(n0, tiles)
-
-        def invert(n0, tiles):
-            cols = slice(n0, n0 + tiles)
-            nc.vector.reciprocal(out=rinv[:, cols], in_=rms[:, cols])
 
         def normalise(g):
             n0, tiles = tiles_of(g)
@@ -263,7 +260,7 @@ def tile_ringattention_pa_t_kernel(tc, x, rotary_emb, gamma, w_qkv, out_0, out_1
             v_bank_of[g] = v_bank
 
         def shared(g):
-            return (1 if 2 < g < N_GROUPS - 4 else 0) if tiles_of(g)[1] == GROUP else 0
+            return (1 if 1 < g < N_GROUPS - 3 else 0) if tiles_of(g)[1] == GROUP else 0
 
         def multiply(engine, g, i, tiles, rot):
             b, t = where(tiles_of(g)[0])
@@ -309,14 +306,16 @@ def tile_ringattention_pa_t_kernel(tc, x, rotary_emb, gamma, w_qkv, out_0, out_1
             b, t = where(n0)
             products = products_of.pop(g)
             qk_out = results.tile([P, SECTIONS, GROUP, HEAD_DIM], F32)
-            adder = nc.vector if g == N_GROUPS - 1 else nc.gpsimd
+            cut = tiles if g < N_GROUPS - 3 else (PAIR if g == N_GROUPS - 3 else (tiles if g == N_GROUPS - 2 else 0))
             halves = products[:].rearrange("p c i (g f e) -> p c i g f e", g=SECTIONS, f=2)
-            adder.tensor_tensor(
-                out=qk_out[:, :, 0:tiles, :].rearrange("p g i (f e) -> p i g f e", f=2),
-                in0=halves[:, 0, 0:tiles, :, :, :],
-                in1=halves[:, 1, 0:tiles, :, ::-1, :],
-                op=ALU.add,
-            )
+            for adder, lo, hi in ((nc.gpsimd, 0, cut), (nc.vector, cut, tiles)):
+                if lo < hi:
+                    adder.tensor_tensor(
+                        out=qk_out[:, :, lo:hi, :].rearrange("p g i (f e) -> p i g f e", f=2),
+                        in0=halves[:, 0, lo:hi, :, :, :],
+                        in1=halves[:, 1, lo:hi, :, ::-1, :],
+                        op=ALU.add,
+                    )
             ts = slice(t, t + tiles)
             nc.sync.dma_start(out=q_rows[b, :, :, ts, :], in_=qk_out[:, 0:HEADS, 0:tiles, :])
             nc.sync.dma_start(out=k_rows[b, :, :, ts, :], in_=qk_out[:, HEADS:, 0:tiles, :])
@@ -336,14 +335,12 @@ def tile_ringattention_pa_t_kernel(tc, x, rotary_emb, gamma, w_qkv, out_0, out_1
                 root(0, 8)
         root(8, EARLY_TILES - 8)
         group_weights()
-        invert(0, 8)
         normalise(0)
         normalise(1)
         regroup(0, 0)
         regroup(1, 0)
         quantise_weights()
         take_magnitudes()
-        invert(8, EARLY_TILES - 8)
         normalise(2)
         fill_table(0)
         quantise(0)
@@ -387,9 +384,7 @@ def tile_ringattention_pa_t_kernel(tc, x, rotary_emb, gamma, w_qkv, out_0, out_1
             if g + 2 < N_GROUPS:
                 regroup(g + 2, 1)
             rotate(g)
-            if g + 3 < N_GROUPS:
-                invert(*tiles_of(g + 3))
-        add_and_store(last - 1)
         copy_out(last)
+        add_and_store(last - 1)
         rotate(last)
         add_and_store(last)

@@ -50,7 +50,7 @@ def tile_ringattention_pa_t_kernel(tc, x, rotary_emb, gamma, w_qkv, out_0, out_1
         psum_keep = stack.enter_context(tc.psum_pool(name="psum_keep", bufs=1))
         psum_t = stack.enter_context(tc.psum_pool(name="psum_t", bufs=2))
         psum_rot = stack.enter_context(tc.psum_pool(name="psum_rot", bufs=3))
-        psum_v = stack.enter_context(tc.psum_pool(name="psum_v", bufs=2))
+        psum_s = stack.enter_context(tc.psum_pool(name="psum_s", bufs=2))
         stack.enter_context(tc.manual_schedule())
 
         def where(n):
@@ -149,7 +149,7 @@ def tile_ringattention_pa_t_kernel(tc, x, rotary_emb, gamma, w_qkv, out_0, out_1
             )
 
         transposed_of, grouped_of, operand_of = {}, {}, {}
-        banks_of, v_bank_of, products_of = {}, {}, {}
+        banks_of, v_bank_of, s_bank_of, products_of = {}, {}, {}, {}
 
         def scalar_sum(n):
             b, t = where(n)
@@ -234,18 +234,27 @@ def tile_ringattention_pa_t_kernel(tc, x, rotary_emb, gamma, w_qkv, out_0, out_1
             )
             operand_of[g] = (codes, scales)
 
+        def scalar_bank():
+            s_bank = psum_s.tile([P, GROUP, INNER], F32)
+            return s_bank
+
         def project(g):
             n0, tiles = tiles_of(g)
             codes, scales = operand_of.pop(g)
-            v_bank = psum_v.tile([P, GROUP, INNER], F32)
+            v_bank = scalar_bank()
             banks_of[g] = []
+            if shared(g):
+                s_bank_of[g] = scalar_bank()
             for i in range(tiles):
                 rows = slice(i * P, (i + 1) * P)
                 if i % PAIR == 0:
                     bank = psum_rot.tile([P, PAIR, ROT_COLS], F32)
                     banks_of[g].append(bank)
+                rot = bank[:, i % PAIR, :]
+                if i >= tiles - shared(g):
+                    rot = s_bank_of[g][:, 0:PAIR, :].rearrange("p a n -> p (a n)")
                 for out, cols in (
-                    (bank[:, i % PAIR, :], slice(0, ROT_COLS)),
+                    (rot, slice(0, ROT_COLS)),
                     (v_bank[:, i, :], slice(ROT_COLS, ROT_COLS + INNER)),
                 ):
                     nc.tensor.matmul_mx(
@@ -278,7 +287,9 @@ def tile_ringattention_pa_t_kernel(tc, x, rotary_emb, gamma, w_qkv, out_0, out_1
             if shared(g):
                 n_s = shared(g)
                 copied = work.tile([P, PAIR, ROT_COLS], F32)
-                nc.scalar.copy(out=copied[:, 0:n_s, :], in_=banks_of[g][1][:, PAIR - n_s :, :])
+                nc.scalar.copy(
+                    out=copied[:, 0, :], in_=s_bank_of.pop(g)[:, 0:PAIR, :].rearrange("p a n -> p (a n)")
+                )
                 multiply(nc.gpsimd, g, GROUP - n_s, n_s, copied[:, 0:n_s, :])
 
         def copy_v(g):

@@ -63,9 +63,9 @@ def tile_ringattention_pa_t_kernel(tc, x, rotary_emb, gamma, w_qkv, out_0, out_1
 
         x_all = keep.tile([P, BATCH, POS_PER_PART, DIM], BF16)
 
-        def load_x(n):
+        def load_x(n, tiles=PAIR):
             b, t = where(n)
-            nc.sync.dma_start(out=x_all[:, b, t : t + PAIR, :], in_=x_rows[b, :, t : t + PAIR, :])
+            nc.sync.dma_start(out=x_all[:, b, t : t + tiles, :], in_=x_rows[b, :, t : t + tiles, :])
 
         load_x(0)
         load_x(2)
@@ -74,14 +74,18 @@ def tile_ringattention_pa_t_kernel(tc, x, rotary_emb, gamma, w_qkv, out_0, out_1
         nc.sync.dma_start(out=gamma_row[0:1, :], in_=gamma.rearrange("(o k) -> o k", o=1))
         load_x(4)
         load_x(6)
-        for n in range(8, EARLY_TILES, PAIR):
-            load_x(n)
+        for n in range(8, EARLY_TILES, GROUP):
+            load_x(n, GROUP)
         w_raw = keep.tile([P, PACK, 3 * INNER], BF16)
         nc.sync.dma_start(out=w_raw[:], in_=w_qkv.rearrange("(p j) n -> p j n", j=PACK))
         angles = keep.tile([P, POS_PER_PART, HEAD_DIM], BF16)
         nc.sync.dma_start(out=angles[:], in_=angle_rows)
-        for n in range(EARLY_TILES, TILES, PAIR):
-            load_x(n)
+        for n in range(EARLY_TILES, TILES, BATCH * GROUP):
+            b, t = where(n)
+            nc.sync.dma_start(
+                out=x_all[:, :, t : t + GROUP, :],
+                in_=x_rows[:, :, t : t + GROUP, :].rearrange("b p t k -> p b t k"),
+            )
 
         ident = keep.tile([P, P], F32)
         make_identity(nc, ident[:])
@@ -282,7 +286,7 @@ def tile_ringattention_pa_t_kernel(tc, x, rotary_emb, gamma, w_qkv, out_0, out_1
             )
 
         def copy_t(g):
-            products = results.tile([P, 2, GROUP, ROT_COLS], F32)
+            products = results.tile([P, 2, GROUP, ROT_COLS], F32, bufs=5)
             products_of[g] = products
             if shared(g):
                 n_s = shared(g)

@@ -136,12 +136,12 @@ def tile_ringattention_pa_t_kernel(tc, x, rotary_emb, gamma, w_qkv, out_0, out_1
 
         def fill_table(t0):
             ts = slice(t0, t0 + TABLE_CHUNK)
-            nc.scalar.activation(
-                out=table[:, ts, 0, 1, :], in_=magnitudes[:, ts, :], func=ACT.Sin, scale=-1.0, bias=math.pi / 2
-            )
             nc.scalar.activation(out=table[:, ts, 1, 1, 0:HALF], in_=angles[:, ts, HALF:], func=ACT.Sin)
             nc.scalar.activation(
                 out=table[:, ts, 1, 1, HALF:], in_=angles[:, ts, 0:HALF], func=ACT.Sin, scale=-1.0
+            )
+            nc.scalar.activation(
+                out=table[:, ts, 0, 1, :], in_=magnitudes[:, ts, :], func=ACT.Sin, scale=-1.0, bias=math.pi / 2
             )
             nc.gpsimd.tensor_scalar(
                 out=table[:, ts, :, 0, :],
@@ -354,9 +354,9 @@ def tile_ringattention_pa_t_kernel(tc, x, rotary_emb, gamma, w_qkv, out_0, out_1
         normalise(1)
         regroup(0, 0)
         regroup(1, 0)
+        normalise(2)
         quantise_weights()
         take_magnitudes()
-        normalise(2)
         fill_table(0)
         quantise(0)
         project(0)

import math
from contextlib import ExitStack

import concourse.mybir as mybir
from concourse.masks import make_identity

F32 = mybir.dt.float32
BF16 = mybir.dt.bfloat16
I32 = mybir.dt.int32
U32 = mybir.dt.uint32
U8 = mybir.dt.uint8
FP8X4 = mybir.dt.float8_e4m3fn_x4
ALU = mybir.AluOpType
ACT = mybir.ActivationFunctionType

P = 128
BATCH, SEQ, DIM = 2, 4096, 512
HEADS, HEAD_DIM = 2, 64
HALF = HEAD_DIM // 2
INNER = HEADS * HEAD_DIM
ROT_COLS = 2 * INNER
SECTIONS = ROT_COLS // HEAD_DIM
PACK = 4
POS_PER_PART = SEQ // P
TILES = BATCH * POS_PER_PART
PAIR = 2
GROUP = 4
GROUP_SIZES = [PAIR, PAIR] + [GROUP] * (TILES // GROUP - 2) + [PAIR, PAIR]
N_GROUPS = len(GROUP_SIZES)
EARLY_TILES = 16
TABLE_CHUNK = 8
FLOOR = 1e-12 * 1e-12 / DIM

FLOPS = 2 * BATCH * SEQ * DIM * 3 * INNER


def tile_ringattention_pa_t_kernel(tc, x, rotary_emb, gamma, w_qkv, out_0, out_1, out_2):
    nc = tc.nc
    x_rows = x.rearrange("b (p t) k -> b p t k", t=POS_PER_PART)
    angle_rows = rotary_emb.rearrange("(p t) d -> p t d", t=POS_PER_PART)
    q_rows = out_0.rearrange("b h (p t) d -> b p h t d", t=POS_PER_PART)
    k_rows = out_1.rearrange("b h (p t) d -> b p h t d", t=POS_PER_PART)
    v_rows = out_2.rearrange("b h (p t) d -> b p h t d", t=POS_PER_PART)

    with ExitStack() as stack:
        keep = stack.enter_context(tc.tile_pool(name="keep", bufs=1))
        small = stack.enter_context(tc.tile_pool(name="small", bufs=4))
        work = stack.enter_context(tc.tile_pool(name="work", bufs=3))
        results = stack.enter_context(tc.tile_pool(name="results", bufs=3))
        psum_keep = stack.enter_context(tc.psum_pool(name="psum_keep", bufs=1))
        psum_t = stack.enter_context(tc.psum_pool(name="psum_t", bufs=2))
        psum_rot = stack.enter_context(tc.psum_pool(name="psum_rot", bufs=3))
        psum_s = stack.enter_context(tc.psum_pool(name="psum_s", bufs=2))
        stack.enter_context(tc.manual_schedule())

        def where(n):
            c, b = divmod(n // GROUP, BATCH)
            return b, c * GROUP + n % GROUP

        def tiles_of(g):
            n0 = sum(GROUP_SIZES[:g])
            return n0, GROUP_SIZES[g]

        x_all = keep.tile([P, BATCH, POS_PER_PART, DIM], BF16)

        def load_x(n, tiles=PAIR):
            b, t = where(n)
            nc.sync.dma_start(out=x_all[:, b, t : t + tiles, :], in_=x_rows[b, :, t : t + tiles, :])

        load_x(0)
        load_x(2)
        gamma_row = keep.tile([P, DIM], BF16)
        nc.vector.memset(gamma_row[:], 0.0)
        nc.sync.dma_start(out=gamma_row[0:1, :], in_=gamma.rearrange("(o k) -> o k", o=1))
        load_x(4)
        load_x(6)
        for n in range(8, EARLY_TILES, GROUP):
            load_x(n, GROUP)
        w_raw = keep.tile([P, PACK, 3 * INNER], BF16)
        nc.sync.dma_start(out=w_raw[:], in_=w_qkv.rearrange("(p j) n -> p j n", j=PACK))
        angles = keep.tile([P, POS_PER_PART, HEAD_DIM], BF16)
        nc.sync.dma_start(out=angles[:], in_=angle_rows)
        for n in range(EARLY_TILES, TILES, BATCH * GROUP):
            b, t = where(n)
            nc.sync.dma_start(
                out=x_all[:, :, t : t + GROUP, :],
                in_=x_rows[:, :, t : t + GROUP, :].rearrange("b p t k -> p b t k"),
            )

        ident = keep.tile([P, P], F32)
        make_identity(nc, ident[:])
        one = keep.tile([P, 1], F32)
        nc.vector.memset(one[:], 1.0)
        nc.scalar.activation(out=one[:], in_=one[:], func=ACT.Abs_reciprocal_sqrt)
        mean_sq = keep.tile([P, TILES], F32)
        above = keep.tile([P, TILES], F32)
        rinv = keep.tile([P, TILES], F32)
        ones = keep.tile([P, P], BF16)
        nc.vector.memset(ones[:], 1.0)
        gamma_all = psum_keep.tile([P, DIM], F32)
        nc.tensor.matmul(out=gamma_all[:], lhsT=ones[:], rhs=gamma_row[:], start=True, stop=True)

        w_codes = keep.tile([P, ROT_COLS + INNER], U32, align_bytes=64)
        w_scales = keep.tile([P, ROT_COLS + INNER], U8, align_bytes=64)
        magnitudes = keep.tile([P, POS_PER_PART, HEAD_DIM], BF16)
        table = keep.tile([P, POS_PER_PART, 2, 2, HEAD_DIM], F32)

        w_grouped = keep.tile([P, ROT_COLS + INNER, PACK], BF16, align_bytes=64)

        def group_weights():
            nc.gpsimd.tensor_scalar(
                out=w_grouped[:],
                in0=w_raw[:].rearrange("p j n -> p n j"),
                scalar1=1.0,
                scalar2=0.0,
                op0=ALU.mult,
                op1=ALU.add,
            )

        def quantise_weights():
            for cols in (slice(0, ROT_COLS), slice(ROT_COLS, ROT_COLS + INNER)):
                nc.vector.quantize_mx(
                    out=w_codes[:, cols].bitcast(FP8X4),
                    scales=w_scales[:, cols],
                    in_=w_grouped[:, cols, :].rearrange("p n j -> p (n j)"),
                )

        def take_magnitudes():
            nc.vector.tensor_scalar(
                out=magnitudes[:].rearrange("p t d -> p (t d)").bitcast(I32),
                in0=angles[:].rearrange("p t d -> p (t d)").bitcast(I32),
                scalar1=0x7FFF7FFF,
                scalar2=None,
                op0=ALU.bitwise_and,
            )

        def fill_table(t0):
            ts = slice(t0, t0 + TABLE_CHUNK)
            nc.scalar.activation(out=table[:, ts, 1, 1, 0:HALF], in_=angles[:, ts, HALF:], func=ACT.Sin)
            nc.scalar.activation(
                out=table[:, ts, 1, 1, HALF:], in_=angles[:, ts, 0:HALF], func=ACT.Sin, scale=-1.0
            )
            nc.scalar.activation(
                out=table[:, ts, 0, 1, :], in_=magnitudes[:, ts, :], func=ACT.Sin, scale=-1.0, bias=math.pi / 2
            )
            nc.gpsimd.tensor_scalar(
                out=table[:, ts, :, 0, :],
                in0=table[:, ts, :, 1, :],
                scalar1=math.sqrt(HEAD_DIM),
                scalar2=0.0,
                op0=ALU.mult,
                op1=ALU.add,
            )

        transposed_of, grouped_of, operand_of = {}, {}, {}
        banks_of, v_bank_of, s_bank_of, products_of = {}, {}, {}, {}

        def scalar_sum(n):
            b, t = where(n)
            junk = small.tile([P, DIM], BF16)
            nc.scalar.activation(
                out=junk[:],
                in_=x_all[:, b, t, :],
                func=ACT.Square,
                scale=1.0 / math.sqrt(DIM),
                accum_out=mean_sq[:, n : n + 1],
            )

        def vector_sum(n):
            b, t = where(n)
            squares = small.tile([P, DIM], BF16)
            nc.vector.scalar_tensor_tensor(
                out=squares[:],
                in0=x_all[:, b, t, :],
                scalar=1.0 / DIM,
                in1=x_all[:, b, t, :],
                op0=ALU.mult,
                op1=ALU.mult,
                accum_out=mean_sq[:, n : n + 1],
            )

        def floor_a(n0, tiles):
            cols = slice(n0, n0 + tiles)
            nc.scalar.activation(out=above[:, cols], in_=mean_sq[:, cols], func=ACT.Relu, bias=-FLOOR)

        def root_b(n0, tiles):
            cols = slice(n0, n0 + tiles)
            nc.scalar.activation(
                out=rinv[:, cols], in_=above[:, cols], func=ACT.Abs_reciprocal_sqrt, bias=FLOOR
            )

        def root(n0, tiles):
            floor_a(n0, tiles)
            root_b(n0, tiles)

        def normalise(g):
            n0, tiles = tiles_of(g)
            transposed_of[g] = []
            for h in range(tiles // PAIR):
                xn = work.tile([P, PAIR, DIM], BF16, bufs=6)
                transposed = psum_t.tile([P, PAIR, 2, P], F32)
                for i in range(PAIR):
                    n = n0 + h * PAIR + i
                    b, t = where(n)
                    nc.vector.scalar_tensor_tensor(
                        out=xn[:, i, :],
                        in0=x_all[:, b, t, :],
                        scalar=rinv[:, n : n + 1],
                        in1=gamma_all[:],
                        op0=ALU.mult,
                        op1=ALU.mult,
                    )
                xn_words = xn[:].bitcast(F32)
                for i in range(PAIR):
                    for u in range(2):
                        nc.tensor.transpose(transposed[:, i, u, :], xn_words[:, i, u : 2 * P : 2], ident[:])
                transposed_of[g].append(transposed)

        def regroup(g, h, copy=nc.scalar.copy):
            n0, tiles = tiles_of(g)
            if h == 0:
                grouped_new = work.tile([P, GROUP, P, PACK], BF16, align_bytes=64)
                grouped_of[g] = grouped_new
            if h < tiles // PAIR:
                copy(
                    out=grouped_of[g][:].bitcast(F32)[:, h * PAIR : (h + 1) * PAIR, :, :],
                    in_=transposed_of[g][h][:].rearrange("p i u r -> p i r u"),
                )

        def quantise(g):
            n0, tiles = tiles_of(g)
            codes = work.tile([P, GROUP * P], U32, align_bytes=64)
            scales = work.tile([P, GROUP * P], U8, align_bytes=64)
            nc.vector.quantize_mx(
                out=codes[:, 0 : tiles * P].bitcast(FP8X4),
                scales=scales[:, 0 : tiles * P],
                in_=grouped_of.pop(g)[:, 0:tiles, :, :].rearrange("p i r j -> p (i r j)"),
            )
            operand_of[g] = (codes, scales)

        def scalar_bank():
            s_bank = psum_s.tile([P, GROUP, INNER], F32)
            return s_bank

        def project(g):
            n0, tiles = tiles_of(g)
            codes, scales = operand_of.pop(g)
            v_bank = scalar_bank()
            banks_of[g] = []
            if shared(g):
                s_bank_of[g] = scalar_bank()
            for i in range(tiles):
                rows = slice(i * P, (i + 1) * P)
                if i % PAIR == 0:
                    bank = psum_rot.tile([P, PAIR, ROT_COLS], F32)
                    banks_of[g].append(bank)
                rot = bank[:, i % PAIR, :]
                if i >= tiles - shared(g):
                    rot = s_bank_of[g][:, 0:PAIR, :].rearrange("p a n -> p (a n)")
                for out, cols in (
                    (rot, slice(0, ROT_COLS)),
                    (v_bank[:, i, :], slice(ROT_COLS, ROT_COLS + INNER)),
                ):
                    nc.tensor.matmul_mx(
                        out=out,
                        lhsT=codes[:, rows].bitcast(FP8X4),
                        lhsT_scale=scales[:, rows],
                        rhs=w_codes[:, cols].bitcast(FP8X4),
                        rhs_scale=w_scales[:, cols],
                        start=True,
                        stop=True,
                    )
            v_bank_of[g] = v_bank

        def shared(g):
            return (1 if 1 < g < N_GROUPS - 3 else 0) if tiles_of(g)[1] == GROUP else 0

        def multiply(engine, g, i, tiles, rot):
            b, t = where(tiles_of(g)[0])
            shape = [P, tiles, 2, 2, HEADS, HEAD_DIM]
            engine.tensor_tensor(
                out=products_of[g][:, :, i : i + tiles, :].rearrange("p c i (q h d) -> p i c q h d", q=2, h=HEADS),
                in0=rot.rearrange("p i (q h d) -> p i q h d", q=2, h=HEADS).unsqueeze(2).to_broadcast(shape),
                in1=table[:, t + i : t + i + tiles, :, :, :].unsqueeze(4).to_broadcast(shape),
                op=ALU.mult,
            )

        def copy_t(g):
            products = results.tile([P, 2, GROUP, ROT_COLS], F32, bufs=5)
            products_of[g] = products
            if shared(g):
                n_s = shared(g)
                copied = work.tile([P, PAIR, ROT_COLS], F32)
                nc.scalar.copy(
                    out=copied[:, 0, :], in_=s_bank_of.pop(g)[:, 0:PAIR, :].rearrange("p a n -> p (a n)")
                )
                multiply(nc.gpsimd, g, GROUP - n_s, n_s, copied[:, 0:n_s, :])

        def copy_v(g):
            n0, tiles = tiles_of(g)
            b, t = where(n0)
            v_out = results.tile([P, HEADS, GROUP, HEAD_DIM], F32)
            nc.scalar.copy(
                out=v_out[:, :, 0:tiles, :].rearrange("p h i d -> p i h d"),
                in_=v_bank_of.pop(g)[:, 0:tiles, :].rearrange("p i (h d) -> p i h d", h=HEADS),
            )
            nc.sync.dma_start(out=v_rows[b, :, :, t : t + tiles, :], in_=v_out[:, :, 0:tiles, :])

        def copy_out(g):
            copy_t(g)
            copy_v(g)

        def rotate(g):
            for h, bank in enumerate(banks_of.pop(g)):
                tiles = PAIR - shared(g) if h == 1 else PAIR
                if tiles > 0:
                    multiply(nc.vector, g, h * PAIR, tiles, bank[:, 0:tiles, :])

        def add_and_store(g):
            n0, tiles = tiles_of(g)
            b, t = where(n0)
            products = products_of.pop(g)
            qk_out = results.tile([P, SECTIONS, GROUP, HEAD_DIM], F32)
            cut = tiles if g < N_GROUPS - 3 else (PAIR if g == N_GROUPS - 3 else (tiles if g == N_GROUPS - 2 else 0))
            halves = products[:].rearrange("p c i (g f e) -> p c i g f e", g=SECTIONS, f=2)
            for adder, lo, hi in ((nc.gpsimd, 0, cut), (nc.vector, cut, tiles)):
                if lo < hi:
                    adder.tensor_tensor(
                        out=qk_out[:, :, lo:hi, :].rearrange("p g i (f e) -> p i g f e", f=2),
                        in0=halves[:, 0, lo:hi, :, :, :],
                        in1=halves[:, 1, lo:hi, :, ::-1, :],
                        op=ALU.add,
                    )
            ts = slice(t, t + tiles)
            nc.sync.dma_start(out=q_rows[b, :, :, ts, :], in_=qk_out[:, 0:HEADS, 0:tiles, :])
            nc.sync.dma_start(out=k_rows[b, :, :, ts, :], in_=qk_out[:, HEADS:, 0:tiles, :])

        def squares(g, lo, hi):
            if g < N_GROUPS:
                n0, tiles = tiles_of(g)
                for n in range(n0 + lo, n0 + min(hi, tiles)):
                    scalar_sum(n)

        for n in range(EARLY_TILES):
            if n % 2 == 1 and n < 12:
                vector_sum(n)
            else:
                scalar_sum(n)
            if n == 7:
                root(0, 8)
        root(8, EARLY_TILES - 8)
        group_weights()
        normalise(0)
        normalise(1)
        regroup(0, 0)
        regroup(1, 0)
        normalise(2)
        quantise_weights()
        take_magnitudes()
        fill_table(0)
        quantise(0)
        project(0)
        quantise(1)
        project(1)
        regroup(2, 0)
        regroup(2, 1)
        normalise(3)
        copy_out(0)
        copy_out(1)
        fill_table(8)
        fill_table(16)
        fill_table(24)
        rotate(0)
        regroup(3, 0, nc.vector.tensor_copy)
        add_and_store(0)
        rotate(1)
        regroup(3, 1, nc.vector.tensor_copy)

        last = N_GROUPS - 1
        for g in range(2, last):
            quantise(g)
            if g == last - 1:
                quantise(last)
            project(g)
            if g == last - 1:
                project(last)
            if g + 2 < N_GROUPS:
                normalise(g + 2)
            add_and_store(g - 1)
            squares(g + 3, 0, 4)
            copy_t(g)
            if g + 3 < N_GROUPS:
                floor_a(*tiles_of(g + 3))
            copy_v(g)
            if g + 3 < N_GROUPS:
                root_b(*tiles_of(g + 3))
            if g + 2 < N_GROUPS:
                regroup(g + 2, 0)
            if g + 2 < N_GROUPS:
                regroup(g + 2, 1)
            rotate(g)
        copy_out(last)
        add_and_store(last - 1)
        rotate(last)
        add_and_store(last)
